import numpy as np
import ml_dtypes


def mxq(x, axis, fmt="e4m3"):
    dtype, down = {"e4m3": (ml_dtypes.float8_e4m3fn, 7), "e5m2": (ml_dtypes.float8_e5m2, 14)}[fmt]
    v = np.moveaxis(np.asarray(x, np.float32).astype(ml_dtypes.bfloat16).astype(np.float64), axis, -1)
    blocks = v.reshape(v.shape[:-1] + (-1, 32))
    amax = np.abs(blocks).max(-1, keepdims=True)
    byte = np.maximum(np.where(amax > 0, np.frexp(amax)[1] - 1 + 127, 0) - down, 1)
    scale = np.exp2(byte - 127.0)
    codes = (blocks / scale).astype(np.float32).astype(dtype).astype(np.float64)
    return np.moveaxis((codes * scale).reshape(v.shape), -1, axis)


WIDE = False


def mx_kscale(k):
    if not WIDE:
        return np.ones(k)
    levels = np.array([10, -10, 5, -5, 0])
    if k % 512:
        return np.exp2(np.random.permutation(np.resize(levels, k // 32))).repeat(32)
    a = np.empty((k // 512, 16))
    for p in range(k // 512):
        a[p, :8] = np.random.permutation(np.resize(levels, 8))
        for g in range(8):
            far = levels[np.abs(levels - a[p, g]) >= 10]
            a[p, g + 8] = far[np.random.randint(len(far))]
    return np.exp2(a.ravel()).repeat(32)


BF16 = ml_dtypes.bfloat16


def bf(x):
    return np.asarray(x, np.float32).astype(BF16)


def f64(x):
    return np.asarray(x).astype(np.float64)


B, SS, SM, SL, N, D = 4, 512, 1024, 1536, 512, 128
T = SS + SM + SL
EPS = 1e-5


def setup_inputs():
    s = mx_kscale(N)
    d = {"x": bf(np.random.standard_normal((B, T, N))),
         "gamma": bf((1.0 + 0.1 * np.random.standard_normal(N)) * s),
         "beta": bf(0.1 * np.random.standard_normal(N) * s)}
    for c in ("s", "m", "l"):
        d["Wqkv_" + c] = bf(np.random.standard_normal((N, 3 * D)) * 1.5 / np.sqrt(N) / s[:, None])
        d["bqkv_" + c] = bf(0.1 * np.random.standard_normal(3 * D))
    return d


def layer_norm(x, gamma, beta):
    mu = x.mean(-1, keepdims=True)
    var = np.square(x - mu).mean(-1, keepdims=True)
    return (x - mu) / np.sqrt(var + EPS) * gamma + beta


def proj(hseg, W, b):
    return (mxq(hseg, 2, "e4m3") @ mxq(f64(W), 0, "e4m3")) + f64(b)


def reference(x, gamma, beta, Wqkv_s, bqkv_s, Wqkv_m, bqkv_m, Wqkv_l, bqkv_l):
    h = layer_norm(f64(x), f64(gamma), f64(beta))
    qkv_s = proj(h[:, :SS], Wqkv_s, bqkv_s)
    qkv_m = proj(h[:, SS:SS + SM], Wqkv_m, bqkv_m)
    qkv_l = proj(h[:, SS + SM:T], Wqkv_l, bqkv_l)
    return np.concatenate([qkv_s, qkv_m, qkv_l], axis=1)

@@ -1,0 +1,283 @@
+import concourse.mybir as mybir
+from concourse.masks import make_identity
+
+F32 = mybir.dt.float32
+BF16 = mybir.dt.bfloat16
+U32 = mybir.dt.uint32
+U8 = mybir.dt.uint8
+FP8X4 = mybir.dt.float8_e4m3fn_x4
+ACT = mybir.ActivationFunctionType
+ALU = mybir.AluOpType
+
+P = 128
+PACK = 4
+FEATURES = P * PACK
+OUT_COLS = 384
+SLOTS = 4
+GROUP_ROWS = P * SLOTS
+EPS = 1e-5
+GROUPS_PER_SEQUENCE = 6
+FIRST_GROUP_OF_SCALE = (0, 1, 3)
+THIRDS = 3
+WEIGHT_QUANTISE_COLUMNS = ((0, 256), (256, 128))
+MOMENTS_AHEAD = 5
+LOAD_AHEAD = MOMENTS_AHEAD + 2
+
+FLOPS = 2 * 4 * 3072 * FEATURES * OUT_COLS
+
+
+def scale_of_group(g):
+    place = g % GROUPS_PER_SEQUENCE
+    return sum(1 for first in FIRST_GROUP_OF_SCALE[1:] if place >= first)
+
+
+def tile_multiscalesattn_pa_t_kernel(
+    tc, x, gamma, beta, Wqkv_s, bqkv_s, Wqkv_m, bqkv_m, Wqkv_l, bqkv_l, out
+):
+    nc = tc.nc
+    weights = (Wqkv_s, Wqkv_m, Wqkv_l)
+    biases = (bqkv_s, bqkv_m, bqkv_l)
+    x_rows = x.flatten_outer_dims()
+    out_rows = out.flatten_outer_dims()
+    groups = x_rows.shape[0] // GROUP_ROWS
+
+    with (
+        tc.tile_pool(name="const", bufs=1) as const,
+        tc.tile_pool(name="x_pool", bufs=6) as x_pool,
+        tc.tile_pool(name="small", bufs=4) as small,
+        tc.tile_pool(name="work", bufs=2) as work,
+        tc.tile_pool(name="out_pool", bufs=9) as out_pool,
+        tc.psum_pool(name="psum", bufs=1) as psum,
+        tc.manual_schedule(),
+    ):
+        x_tiles = {}
+        moments = {}
+        row_scalars = {}
+        normalised = {}
+        transposed = {}
+        plane_tiles = {}
+        grouped_tiles = {}
+        h_operands = {}
+        sums = {}
+
+        identity = const.tile([P, P], F32, name="identity")
+        make_identity(nc, identity[:])
+
+        w_raw = [const.tile([P, PACK, OUT_COLS], BF16, name="w_raw%d" % c) for c in range(3)]
+        w_grouped = [
+            const.tile([P, OUT_COLS, PACK], BF16, name="w_grouped%d" % c, align_bytes=64)
+            for c in range(3)
+        ]
+        w_codes = const.tile([P, 3, OUT_COLS], U32, name="w_codes", align_bytes=64)
+        w_scales = const.tile([P, 3, OUT_COLS], U8, name="w_scales", align_bytes=64)
+        bias_all_rows = [const.tile([P, OUT_COLS], BF16, name="bias%d" % c) for c in range(3)]
+
+        eps_col = const.tile([P, 1], F32, name="eps_col")
+        nc.vector.memset(eps_col[:], EPS)
+
+        def load_x(g):
+            x_tiles[g] = x_pool.tile([P, SLOTS, FEATURES], BF16, name="x_sb")
+            rows = x_rows[g * GROUP_ROWS : (g + 1) * GROUP_ROWS, :]
+            by_slot = rows.rearrange("(p j) f -> p j f", j=SLOTS)
+            if g == 0:
+                for j in range(SLOTS):
+                    nc.sync.dma_start(out=x_tiles[g][:, j, :], in_=by_slot[:, j, :])
+            else:
+                nc.sync.dma_start(out=x_tiles[g][:], in_=by_slot)
+
+        def load_weight(c):
+            nc.sync.dma_start(
+                out=w_raw[c][:], in_=weights[c].rearrange("(p t) n -> p t n", t=PACK)
+            )
+
+        def group_weight(c):
+            nc.scalar.copy(
+                out=w_grouped[c][:].rearrange("p (n i) t -> p n t i", i=4),
+                in_=w_raw[c][:].rearrange("p t (n i) -> p n t i", i=4),
+            )
+
+        def quantise_weight(c):
+            flat = w_grouped[c][:].rearrange("p n t -> p (n t)")
+            for first, width in WEIGHT_QUANTISE_COLUMNS:
+                nc.vector.quantize_mx(
+                    out=w_codes[:, c, first : first + width].bitcast(FP8X4),
+                    scales=w_scales[:, c, first : first + width],
+                    in_=flat[:, first * PACK : (first + width) * PACK],
+                )
+
+        load_x(0)
+
+        gamma_raw = const.tile([P, PACK], BF16, name="gamma_raw")
+        beta_raw = const.tile([P, PACK], BF16, name="beta_raw")
+        gamma_cols = const.tile([P, PACK], F32, name="gamma_cols")
+        beta_cols = const.tile([P, PACK], F32, name="beta_cols")
+        nc.sync.dma_start(out=gamma_raw[:], in_=gamma.rearrange("(p t) -> p t", t=PACK))
+        nc.sync.dma_start(out=beta_raw[:], in_=beta.rearrange("(p t) -> p t", t=PACK))
+
+        def spread_gamma_beta():
+            nc.vector.tensor_copy(out=gamma_cols[:], in_=gamma_raw[:])
+            nc.vector.tensor_copy(out=beta_cols[:], in_=beta_raw[:])
+
+        load_weight(0)
+        load_x(1)
+        load_weight(1)
+        load_x(2)
+        load_weight(2)
+        for c in range(3):
+            nc.sync.dma_start(out=bias_all_rows[c][:], in_=biases[c].partition_broadcast(P))
+        load_x(3)
+        preloaded = 4
+
+        def row_moments(g):
+            stats = small.tile([P, SLOTS, 6], F32, name="stats")
+            mean_var = small.tile([P, SLOTS, 2], F32, name="mean_var")
+            for j in range(SLOTS):
+                nc.vector.bn_stats(out=stats[:, j, :], in_=x_tiles[g][:, j, :])
+            for j in range(SLOTS):
+                nc.vector.bn_aggr(out=mean_var[:, j, :], in_=stats[:, j, :])
+            moments[g] = mean_var
+
+        def row_scalars_of(g):
+            mean_var = moments[g]
+            std = small.tile([P, SLOTS], F32, name="std")
+            rstd = small.tile([P, SLOTS], F32, name="rstd")
+            neg_mean = small.tile([P, SLOTS], F32, name="neg_mean")
+            nc.scalar.activation(
+                out=std[:], in_=mean_var[:, :, 1], func=ACT.Sqrt, bias=eps_col[:]
+            )
+            nc.scalar.mul(out=neg_mean[:], in_=mean_var[:, :, 0], mul=-1.0)
+            nc.vector.reciprocal(out=rstd[:], in_=std[:])
+            row_scalars[g] = (neg_mean, rstd)
+
+        def normalise(g):
+            neg_mean, rstd = row_scalars[g]
+            x_sb = x_tiles[g]
+            xn = work.tile([P, SLOTS, FEATURES], F32, name="xn")
+            for j in range(SLOTS):
+                nc.gpsimd.tensor_scalar(
+                    out=xn[:, j, :].rearrange("p (t q) -> p t q", t=PACK),
+                    in0=x_sb[:, j, :].rearrange("p (q t) -> p t q", t=PACK),
+                    scalar1=neg_mean[:, j : j + 1],
+                    scalar2=rstd[:, j : j + 1],
+                    op0=ALU.add,
+                    op1=ALU.mult,
+                )
+            normalised[g] = xn
+
+        def transpose_group(g):
+            xn = normalised[g]
+            banks = []
+            for t in range(PACK):
+                bank = psum.tile([P, GROUP_ROWS], F32, name="transposed%d" % t)
+                for j in range(SLOTS):
+                    nc.tensor.transpose(
+                        out=bank[:, j * P : (j + 1) * P],
+                        in_=xn[:, j, t * P : (t + 1) * P],
+                        identity=identity[:],
+                    )
+                banks.append(bank)
+            transposed[g] = banks
+
+        def scale_shift_group(g):
+            banks = transposed[g]
+            planes = work.tile([P, PACK, GROUP_ROWS], BF16, name="planes")
+            for t in range(PACK):
+                nc.scalar.activation(
+                    out=planes[:, t, :],
+                    in_=banks[t][:],
+                    func=ACT.Identity,
+                    scale=gamma_cols[:, t : t + 1],
+                    bias=beta_cols[:, t : t + 1],
+                )
+            plane_tiles[g] = planes
+
+        def group_words(g):
+            planes = plane_tiles[g]
+            grouped = work.tile([P, GROUP_ROWS, PACK], BF16, name="grouped", align_bytes=64)
+            grouped_runs = grouped[:].rearrange("p (c i) t -> p c t i", i=4)
+            plane_runs = planes[:].rearrange("p t (c i) -> p c t i", i=4)
+            if g - 1 + MOMENTS_AHEAD < groups:
+                nc.scalar.copy(out=grouped_runs, in_=plane_runs)
+            else:
+                nc.vector.tensor_copy(out=grouped_runs, in_=plane_runs)
+            grouped_tiles[g] = grouped
+
+        def quantise_group(g):
+            grouped = grouped_tiles[g]
+            codes = work.tile([P, GROUP_ROWS], U32, name="codes", align_bytes=64)
+            scales = work.tile([P, GROUP_ROWS], U8, name="scales", align_bytes=64)
+            nc.vector.quantize_mx(
+                out=codes[:].bitcast(FP8X4),
+                scales=scales[:],
+                in_=grouped[:].rearrange("p c t -> p (c t)"),
+            )
+            h_operands[g] = (codes, scales)
+
+        def project_group(g):
+            codes, scales = h_operands[g]
+            c = scale_of_group(g)
+            banks = [psum.tile([P, SLOTS, P], F32, name="sums%d" % b) for b in range(THIRDS)]
+            for b in range(THIRDS):
+                for j in range(SLOTS):
+                    nc.tensor.matmul_mx(
+                        out=banks[b][:, j, :],
+                        lhsT=codes[:, j * P : (j + 1) * P].bitcast(FP8X4),
+                        lhsT_scale=scales[:, j * P : (j + 1) * P],
+                        rhs=w_codes[:, c, b * P : (b + 1) * P].bitcast(FP8X4),
+                        rhs_scale=w_scales[:, c, b * P : (b + 1) * P],
+                        start=True,
+                        stop=True,
+                    )
+            sums[g] = banks
+
+        def add_bias_and_store(g):
+            c = scale_of_group(g)
+            rows = out_rows[g * GROUP_ROWS : (g + 1) * GROUP_ROWS, :]
+            for b in range(THIRDS):
+                result = out_pool.tile([P, SLOTS, P], F32, name="result")
+                bias_block = bias_all_rows[c][:, b * P : (b + 1) * P]
+                nc.vector.tensor_tensor(
+                    out=result[:],
+                    in0=sums[g][b][:],
+                    in1=bias_block.unsqueeze(1).to_broadcast([P, SLOTS, P]),
+                    op=ALU.add,
+                )
+                nc.sync.dma_start(
+                    out=rows[:, b * P : (b + 1) * P].rearrange("(p j) n -> p j n", j=SLOTS),
+                    in_=result[:],
+                )
+
+        def in_range(g):
+            return 0 <= g < groups
+
+        row_moments(0)
+        row_scalars_of(0)
+        normalise(0)
+        spread_gamma_beta()
+        row_moments(1)
+
+        for step in range(-3, groups + 1):
+            if preloaded <= step + LOAD_AHEAD < groups:
+                load_x(step + LOAD_AHEAD)
+            if step < 0:
+                group_weight(step + 3)
+            if step == 0:
+                for c in range(3):
+                    quantise_weight(c)
+            if in_range(step):
+                quantise_group(step)
+            if 0 < step + 3 < groups:
+                row_scalars_of(step + 3)
+                normalise(step + 3)
+            if in_range(step - 1):
+                add_bias_and_store(step - 1)
+            if in_range(step + 1):
+                scale_shift_group(step + 1)
+            if in_range(step + 2):
+                transpose_group(step + 2)
+            if in_range(step + 1):
+                group_words(step + 1)
+            if in_range(step):
+                project_group(step)
+            if in_range(step + MOMENTS_AHEAD):
+                row_moments(step + MOMENTS_AHEAD)

@@ -155,8 +155,8 @@ def tile_multiscalesattn_pa_t_kernel(
             xn = work.tile([P, SLOTS, FEATURES], F32, name="xn")
             for j in range(SLOTS):
                 nc.gpsimd.tensor_scalar(
-                    out=xn[:, j, :].rearrange("p (t q) -> p t q", t=PACK),
-                    in0=x_sb[:, j, :].rearrange("p (q t) -> p t q", t=PACK),
+                    out=xn[:, j, :],
+                    in0=x_sb[:, j, :],
                     scalar1=neg_mean[:, j : j + 1],
                     scalar2=rstd[:, j : j + 1],
                     op0=ALU.add,
@@ -172,7 +172,7 @@ def tile_multiscalesattn_pa_t_kernel(
                 for j in range(SLOTS):
                     nc.tensor.transpose(
                         out=bank[:, j * P : (j + 1) * P],
-                        in_=xn[:, j, t * P : (t + 1) * P],
+                        in_=xn[:, j, t::PACK],
                         identity=identity[:],
                     )
                 banks.append(bank)

@@ -20,6 +20,7 @@ GROUPS_PER_SEQUENCE = 6
 FIRST_GROUP_OF_SCALE = (0, 1, 3)
 THIRDS = 3
 WEIGHT_QUANTISE_COLUMNS = ((0, 256), (256, 128))
+VECTOR_WORDS_LAST = 1
 MOMENTS_AHEAD = 5
 LOAD_AHEAD = MOMENTS_AHEAD + 2
 
@@ -196,7 +197,7 @@ def tile_multiscalesattn_pa_t_kernel(
             grouped = work.tile([P, GROUP_ROWS, PACK], BF16, name="grouped", align_bytes=64)
             grouped_runs = grouped[:].rearrange("p (c i) t -> p c t i", i=4)
             plane_runs = planes[:].rearrange("p t (c i) -> p c t i", i=4)
-            if g - 1 + MOMENTS_AHEAD < groups:
+            if g < groups - VECTOR_WORDS_LAST:
                 nc.scalar.copy(out=grouped_runs, in_=plane_runs)
             else:
                 nc.vector.tensor_copy(out=grouped_runs, in_=plane_runs)

@@ -195,8 +195,8 @@ def tile_multiscalesattn_pa_t_kernel(
         def group_words(g):
             planes = plane_tiles[g]
             grouped = work.tile([P, GROUP_ROWS, PACK], BF16, name="grouped", align_bytes=64)
-            grouped_runs = grouped[:].rearrange("p (c i) t -> p c t i", i=4)
-            plane_runs = planes[:].rearrange("p t (c i) -> p c t i", i=4)
+            grouped_runs = grouped[:].rearrange("p (c i) t -> p c t i", i=8)
+            plane_runs = planes[:].rearrange("p t (c i) -> p c t i", i=8)
             if g < groups - VECTOR_WORDS_LAST:
                 nc.scalar.copy(out=grouped_runs, in_=plane_runs)
             else:

@@ -45,9 +45,9 @@ def tile_multiscalesattn_pa_t_kernel(
     with (
         tc.tile_pool(name="const", bufs=1) as const,
         tc.tile_pool(name="x_pool", bufs=6) as x_pool,
-        tc.tile_pool(name="small", bufs=4) as small,
-        tc.tile_pool(name="work", bufs=2) as work,
-        tc.tile_pool(name="out_pool", bufs=9) as out_pool,
+        tc.tile_pool(name="small", bufs=24) as small,
+        tc.tile_pool(name="work", bufs=3) as work,
+        tc.tile_pool(name="out_pool", bufs=18) as out_pool,
         tc.psum_pool(name="psum", bufs=1) as psum,
         tc.manual_schedule(),
     ):
@@ -75,6 +75,8 @@ def tile_multiscalesattn_pa_t_kernel(
 
         eps_col = const.tile([P, 1], F32, name="eps_col")
         nc.vector.memset(eps_col[:], EPS)
+        first_root = const.tile([P, 1], F32, name="first_root")
+        nc.scalar.activation(out=first_root[:], in_=eps_col[:], func=ACT.Sqrt)
 
         def load_x(g):
             x_tiles[g] = x_pool.tile([P, SLOTS, FEATURES], BF16, name="x_sb")
@@ -143,10 +145,10 @@ def tile_multiscalesattn_pa_t_kernel(
             std = small.tile([P, SLOTS], F32, name="std")
             rstd = small.tile([P, SLOTS], F32, name="rstd")
             neg_mean = small.tile([P, SLOTS], F32, name="neg_mean")
+            nc.scalar.mul(out=neg_mean[:], in_=mean_var[:, :, 0], mul=-1.0)
             nc.scalar.activation(
                 out=std[:], in_=mean_var[:, :, 1], func=ACT.Sqrt, bias=eps_col[:]
             )
-            nc.scalar.mul(out=neg_mean[:], in_=mean_var[:, :, 0], mul=-1.0)
             nc.vector.reciprocal(out=rstd[:], in_=std[:])
             row_scalars[g] = (neg_mean, rstd)
 
@@ -233,20 +235,22 @@ def tile_multiscalesattn_pa_t_kernel(
 
         def add_bias_and_store(g):
             c = scale_of_group(g)
-            rows = out_rows[g * GROUP_ROWS : (g + 1) * GROUP_ROWS, :]
+            rows = out_rows[g * GROUP_ROWS : (g + 1) * GROUP_ROWS, :].rearrange(
+                "(p j) n -> p j n", j=SLOTS
+            )
+            result = out_pool.tile([P, SLOTS, OUT_COLS], F32, name="result")
             for b in range(THIRDS):
-                result = out_pool.tile([P, SLOTS, P], F32, name="result")
-                bias_block = bias_all_rows[c][:, b * P : (b + 1) * P]
+                own = slice(b * P, (b + 1) * P)
                 nc.vector.tensor_tensor(
-                    out=result[:],
+                    out=result[:, :, own],
                     in0=sums[g][b][:],
-                    in1=bias_block.unsqueeze(1).to_broadcast([P, SLOTS, P]),
+                    in1=bias_all_rows[c][:, own].unsqueeze(1).to_broadcast([P, SLOTS, P]),
                     op=ALU.add,
                 )
-                nc.sync.dma_start(
-                    out=rows[:, b * P : (b + 1) * P].rearrange("(p j) n -> p j n", j=SLOTS),
-                    in_=result[:],
-                )
+                if g == groups - 1:
+                    nc.sync.dma_start(out=rows[:, :, own], in_=result[:, :, own])
+            if g < groups - 1:
+                nc.sync.dma_start(out=rows, in_=result[:])
 
         def in_range(g):
             return 0 <= g < groups

@@ -76,7 +76,7 @@ def tile_multiscalesattn_pa_t_kernel(
         eps_col = const.tile([P, 1], F32, name="eps_col")
         nc.vector.memset(eps_col[:], EPS)
         first_root = const.tile([P, 1], F32, name="first_root")
-        nc.scalar.activation(out=first_root[:], in_=eps_col[:], func=ACT.Sqrt)
+        nc.scalar.activation(out=first_root[:], in_=eps_col[:], func=ACT.Abs_reciprocal_sqrt)
 
         def load_x(g):
             x_tiles[g] = x_pool.tile([P, SLOTS, FEATURES], BF16, name="x_sb")
@@ -142,14 +142,15 @@ def tile_multiscalesattn_pa_t_kernel(
 
         def row_scalars_of(g):
             mean_var = moments[g]
-            std = small.tile([P, SLOTS], F32, name="std")
             rstd = small.tile([P, SLOTS], F32, name="rstd")
             neg_mean = small.tile([P, SLOTS], F32, name="neg_mean")
             nc.scalar.mul(out=neg_mean[:], in_=mean_var[:, :, 0], mul=-1.0)
             nc.scalar.activation(
-                out=std[:], in_=mean_var[:, :, 1], func=ACT.Sqrt, bias=eps_col[:]
+                out=rstd[:],
+                in_=mean_var[:, :, 1],
+                func=ACT.Abs_reciprocal_sqrt,
+                bias=eps_col[:],
             )
-            nc.vector.reciprocal(out=rstd[:], in_=std[:])
             row_scalars[g] = (neg_mean, rstd)
 
         def normalise(g):
@@ -266,9 +267,8 @@ def tile_multiscalesattn_pa_t_kernel(
                 load_x(step + LOAD_AHEAD)
             if step < 0:
                 group_weight(step + 3)
-            if step == 0:
-                for c in range(3):
-                    quantise_weight(c)
+            if 0 <= step < 3:
+                quantise_weight(step)
             if in_range(step):
                 quantise_group(step)
             if 0 < step + 3 < groups:

import concourse.mybir as mybir
from concourse.masks import make_identity

F32 = mybir.dt.float32
BF16 = mybir.dt.bfloat16
U32 = mybir.dt.uint32
U8 = mybir.dt.uint8
FP8X4 = mybir.dt.float8_e4m3fn_x4
ACT = mybir.ActivationFunctionType
ALU = mybir.AluOpType

P = 128
PACK = 4
FEATURES = P * PACK
OUT_COLS = 384
SLOTS = 4
GROUP_ROWS = P * SLOTS
EPS = 1e-5
GROUPS_PER_SEQUENCE = 6
FIRST_GROUP_OF_SCALE = (0, 1, 3)
THIRDS = 3
WEIGHT_QUANTISE_COLUMNS = ((0, 256), (256, 128))
VECTOR_WORDS_LAST = 1
MOMENTS_AHEAD = 5
LOAD_AHEAD = MOMENTS_AHEAD + 2

FLOPS = 2 * 4 * 3072 * FEATURES * OUT_COLS


def scale_of_group(g):
    place = g % GROUPS_PER_SEQUENCE
    return sum(1 for first in FIRST_GROUP_OF_SCALE[1:] if place >= first)


def tile_multiscalesattn_pa_t_kernel(
    tc, x, gamma, beta, Wqkv_s, bqkv_s, Wqkv_m, bqkv_m, Wqkv_l, bqkv_l, out
):
    nc = tc.nc
    weights = (Wqkv_s, Wqkv_m, Wqkv_l)
    biases = (bqkv_s, bqkv_m, bqkv_l)
    x_rows = x.flatten_outer_dims()
    out_rows = out.flatten_outer_dims()
    groups = x_rows.shape[0] // GROUP_ROWS

    with (
        tc.tile_pool(name="const", bufs=1) as const,
        tc.tile_pool(name="x_pool", bufs=6) as x_pool,
        tc.tile_pool(name="small", bufs=24) as small,
        tc.tile_pool(name="work", bufs=3) as work,
        tc.tile_pool(name="out_pool", bufs=18) as out_pool,
        tc.psum_pool(name="psum", bufs=1) as psum,
        tc.manual_schedule(),
    ):
        x_tiles = {}
        moments = {}
        row_scalars = {}
        normalised = {}
        transposed = {}
        plane_tiles = {}
        grouped_tiles = {}
        h_operands = {}
        sums = {}

        identity = const.tile([P, P], F32, name="identity")
        make_identity(nc, identity[:])

        w_raw = [const.tile([P, PACK, OUT_COLS], BF16, name="w_raw%d" % c) for c in range(3)]
        w_grouped = [
            const.tile([P, OUT_COLS, PACK], BF16, name="w_grouped%d" % c, align_bytes=64)
            for c in range(3)
        ]
        w_codes = const.tile([P, 3, OUT_COLS], U32, name="w_codes", align_bytes=64)
        w_scales = const.tile([P, 3, OUT_COLS], U8, name="w_scales", align_bytes=64)
        bias_all_rows = [const.tile([P, OUT_COLS], BF16, name="bias%d" % c) for c in range(3)]

        eps_col = const.tile([P, 1], F32, name="eps_col")
        nc.vector.memset(eps_col[:], EPS)
        first_root = const.tile([P, 1], F32, name="first_root")
        nc.scalar.activation(out=first_root[:], in_=eps_col[:], func=ACT.Abs_reciprocal_sqrt)

        def load_x(g):
            x_tiles[g] = x_pool.tile([P, SLOTS, FEATURES], BF16, name="x_sb")
            rows = x_rows[g * GROUP_ROWS : (g + 1) * GROUP_ROWS, :]
            by_slot = rows.rearrange("(p j) f -> p j f", j=SLOTS)
            if g == 0:
                for j in range(SLOTS):
                    nc.sync.dma_start(out=x_tiles[g][:, j, :], in_=by_slot[:, j, :])
            else:
                nc.sync.dma_start(out=x_tiles[g][:], in_=by_slot)

        def load_weight(c):
            nc.sync.dma_start(
                out=w_raw[c][:], in_=weights[c].rearrange("(p t) n -> p t n", t=PACK)
            )

        def group_weight(c):
            nc.scalar.copy(
                out=w_grouped[c][:].rearrange("p (n i) t -> p n t i", i=4),
                in_=w_raw[c][:].rearrange("p t (n i) -> p n t i", i=4),
            )

        def quantise_weight(c):
            flat = w_grouped[c][:].rearrange("p n t -> p (n t)")
            for first, width in WEIGHT_QUANTISE_COLUMNS:
                nc.vector.quantize_mx(
                    out=w_codes[:, c, first : first + width].bitcast(FP8X4),
                    scales=w_scales[:, c, first : first + width],
                    in_=flat[:, first * PACK : (first + width) * PACK],
                )

        load_x(0)

        gamma_raw = const.tile([P, PACK], BF16, name="gamma_raw")
        beta_raw = const.tile([P, PACK], BF16, name="beta_raw")
        gamma_cols = const.tile([P, PACK], F32, name="gamma_cols")
        beta_cols = const.tile([P, PACK], F32, name="beta_cols")
        nc.sync.dma_start(out=gamma_raw[:], in_=gamma.rearrange("(p t) -> p t", t=PACK))
        nc.sync.dma_start(out=beta_raw[:], in_=beta.rearrange("(p t) -> p t", t=PACK))

        def spread_gamma_beta():
            nc.vector.tensor_copy(out=gamma_cols[:], in_=gamma_raw[:])
            nc.vector.tensor_copy(out=beta_cols[:], in_=beta_raw[:])

        load_weight(0)
        load_x(1)
        load_weight(1)
        load_x(2)
        load_weight(2)
        for c in range(3):
            nc.sync.dma_start(out=bias_all_rows[c][:], in_=biases[c].partition_broadcast(P))
        load_x(3)
        preloaded = 4

        def row_moments(g):
            stats = small.tile([P, SLOTS, 6], F32, name="stats")
            mean_var = small.tile([P, SLOTS, 2], F32, name="mean_var")
            for j in range(SLOTS):
                nc.vector.bn_stats(out=stats[:, j, :], in_=x_tiles[g][:, j, :])
            for j in range(SLOTS):
                nc.vector.bn_aggr(out=mean_var[:, j, :], in_=stats[:, j, :])
            moments[g] = mean_var

        def row_scalars_of(g):
            mean_var = moments[g]
            rstd = small.tile([P, SLOTS], F32, name="rstd")
            neg_mean = small.tile([P, SLOTS], F32, name="neg_mean")
            nc.scalar.mul(out=neg_mean[:], in_=mean_var[:, :, 0], mul=-1.0)
            nc.scalar.activation(
                out=rstd[:],
                in_=mean_var[:, :, 1],
                func=ACT.Abs_reciprocal_sqrt,
                bias=eps_col[:],
            )
            row_scalars[g] = (neg_mean, rstd)

        def normalise(g):
            neg_mean, rstd = row_scalars[g]
            x_sb = x_tiles[g]
            xn = work.tile([P, SLOTS, FEATURES], F32, name="xn")
            for j in range(SLOTS):
                nc.gpsimd.tensor_scalar(
                    out=xn[:, j, :],
                    in0=x_sb[:, j, :],
                    scalar1=neg_mean[:, j : j + 1],
                    scalar2=rstd[:, j : j + 1],
                    op0=ALU.add,
                    op1=ALU.mult,
                )
            normalised[g] = xn

        def transpose_group(g):
            xn = normalised[g]
            banks = []
            for t in range(PACK):
                bank = psum.tile([P, GROUP_ROWS], F32, name="transposed%d" % t)
                for j in range(SLOTS):
                    nc.tensor.transpose(
                        out=bank[:, j * P : (j + 1) * P],
                        in_=xn[:, j, t::PACK],
                        identity=identity[:],
                    )
                banks.append(bank)
            transposed[g] = banks

        def scale_shift_group(g):
            banks = transposed[g]
            planes = work.tile([P, PACK, GROUP_ROWS], BF16, name="planes")
            for t in range(PACK):
                nc.scalar.activation(
                    out=planes[:, t, :],
                    in_=banks[t][:],
                    func=ACT.Identity,
                    scale=gamma_cols[:, t : t + 1],
                    bias=beta_cols[:, t : t + 1],
                )
            plane_tiles[g] = planes

        def group_words(g):
            planes = plane_tiles[g]
            grouped = work.tile([P, GROUP_ROWS, PACK], BF16, name="grouped", align_bytes=64)
            grouped_runs = grouped[:].rearrange("p (c i) t -> p c t i", i=8)
            plane_runs = planes[:].rearrange("p t (c i) -> p c t i", i=8)
            if g < groups - VECTOR_WORDS_LAST:
                nc.scalar.copy(out=grouped_runs, in_=plane_runs)
            else:
                nc.vector.tensor_copy(out=grouped_runs, in_=plane_runs)
            grouped_tiles[g] = grouped

        def quantise_group(g):
            grouped = grouped_tiles[g]
            codes = work.tile([P, GROUP_ROWS], U32, name="codes", align_bytes=64)
            scales = work.tile([P, GROUP_ROWS], U8, name="scales", align_bytes=64)
            nc.vector.quantize_mx(
                out=codes[:].bitcast(FP8X4),
                scales=scales[:],
                in_=grouped[:].rearrange("p c t -> p (c t)"),
            )
            h_operands[g] = (codes, scales)

        def project_group(g):
            codes, scales = h_operands[g]
            c = scale_of_group(g)
            banks = [psum.tile([P, SLOTS, P], F32, name="sums%d" % b) for b in range(THIRDS)]
            for b in range(THIRDS):
                for j in range(SLOTS):
                    nc.tensor.matmul_mx(
                        out=banks[b][:, j, :],
                        lhsT=codes[:, j * P : (j + 1) * P].bitcast(FP8X4),
                        lhsT_scale=scales[:, j * P : (j + 1) * P],
                        rhs=w_codes[:, c, b * P : (b + 1) * P].bitcast(FP8X4),
                        rhs_scale=w_scales[:, c, b * P : (b + 1) * P],
                        start=True,
                        stop=True,
                    )
            sums[g] = banks

        def add_bias_and_store(g):
            c = scale_of_group(g)
            rows = out_rows[g * GROUP_ROWS : (g + 1) * GROUP_ROWS, :].rearrange(
                "(p j) n -> p j n", j=SLOTS
            )
            result = out_pool.tile([P, SLOTS, OUT_COLS], F32, name="result")
            for b in range(THIRDS):
                own = slice(b * P, (b + 1) * P)
                nc.vector.tensor_tensor(
                    out=result[:, :, own],
                    in0=sums[g][b][:],
                    in1=bias_all_rows[c][:, own].unsqueeze(1).to_broadcast([P, SLOTS, P]),
                    op=ALU.add,
                )
                if g == groups - 1:
                    nc.sync.dma_start(out=rows[:, :, own], in_=result[:, :, own])
            if g < groups - 1:
                nc.sync.dma_start(out=rows, in_=result[:])

        def in_range(g):
            return 0 <= g < groups

        row_moments(0)
        row_scalars_of(0)
        normalise(0)
        spread_gamma_beta()
        row_moments(1)

        for step in range(-3, groups + 1):
            if preloaded <= step + LOAD_AHEAD < groups:
                load_x(step + LOAD_AHEAD)
            if step < 0:
                group_weight(step + 3)
            if 0 <= step < 3:
                quantise_weight(step)
            if in_range(step):
                quantise_group(step)
            if 0 < step + 3 < groups:
                row_scalars_of(step + 3)
                normalise(step + 3)
            if in_range(step - 1):
                add_bias_and_store(step - 1)
            if in_range(step + 1):
                scale_shift_group(step + 1)
            if in_range(step + 2):
                transpose_group(step + 2)
            if in_range(step + 1):
                group_words(step + 1)
            if in_range(step):
                project_group(step)
            if in_range(step + MOMENTS_AHEAD):
                row_moments(step + MOMENTS_AHEAD)
